import numpy as np
import ml_dtypes


def mxq(x, axis, fmt="e4m3"):
    dtype, down = {"e4m3": (ml_dtypes.float8_e4m3fn, 7), "e5m2": (ml_dtypes.float8_e5m2, 14)}[fmt]
    v = np.moveaxis(np.asarray(x, np.float32).astype(ml_dtypes.bfloat16).astype(np.float64), axis, -1)
    blocks = v.reshape(v.shape[:-1] + (-1, 32))
    amax = np.abs(blocks).max(-1, keepdims=True)
    byte = np.maximum(np.where(amax > 0, np.frexp(amax)[1] - 1 + 127, 0) - down, 1)
    scale = np.exp2(byte - 127.0)
    codes = (blocks / scale).astype(np.float32).astype(dtype).astype(np.float64)
    return np.moveaxis((codes * scale).reshape(v.shape), -1, axis)


WIDE = False


def mx_kscale(k):
    if not WIDE:
        return np.ones(k)
    levels = np.array([20, -20, 10, -10, 0])
    a = np.random.permutation(np.resize(levels, k // 512 * 4)).reshape(k // 512, 4)
    idx = np.arange(k)
    return np.exp2(a[idx // 512, idx % 128 // 32])


BF16 = ml_dtypes.bfloat16


def bf(x):
    return np.asarray(x, np.float32).astype(BF16)


def f64(x):
    return np.asarray(x).astype(np.float64)


B, S, NI, NO = 16, 256, 256, 128


def _table(Wr, Wi, Wj, Wk):
    return np.stack([
        np.stack([Wr, -Wi, -Wj, -Wk]),
        np.stack([Wi, Wr, Wk, -Wj]),
        np.stack([Wj, -Wk, Wr, Wi]),
        np.stack([Wk, Wj, -Wi, Wr]),
    ])


def setup_inputs():
    sm = mx_kscale(4 * NO)[::4]
    sc = NI ** -0.5

    def u():
        return bf(np.random.uniform(-sc, sc, (NO, NI)) / sm[:, None])

    q = bf(np.random.standard_normal((B, S, 4 * NI)))
    wr, wi, wj, wk = u(), u(), u(), u()
    g = np.random.standard_normal((B, S, 4 * NO)) * np.exp2(np.random.randint(-12, 1, (B, S, 1))) * 4.0 * np.repeat(sm, 4)
    return {"q_in": q, "r_weight": wr, "i_weight": wi, "j_weight": wj, "k_weight": wk, "grad_out": bf(g)}


def reference(q_in, r_weight, i_weight, j_weight, k_weight, grad_out):
    g = f64(grad_out)
    U = np.stack([f64(r_weight), f64(i_weight), f64(j_weight), f64(k_weight)]).transpose(1, 0, 2).reshape(4 * NO, NI)
    Uq = mxq(U, 0, "e4m3")
    Wr, Wi, Wj, Wk = Uq.reshape(NO, 4, NI).transpose(1, 0, 2)
    W4 = _table(Wr, Wi, Wj, Wk)
    Wt = W4.transpose(2, 0, 3, 1).reshape(4 * NO, 4 * NI)
    return mxq(g, 2, "e5m2") @ Wt

@@ -1,0 +1,145 @@
+from contextlib import ExitStack
+
+import concourse.mybir as mybir
+from concourse.masks import make_identity
+
+F32 = mybir.dt.float32
+BF16 = mybir.dt.bfloat16
+U32 = mybir.dt.uint32
+U8 = mybir.dt.uint8
+E4M3_X4 = mybir.dt.float8_e4m3fn_x4
+E5M2_X4 = mybir.dt.float8_e5m2_x4
+
+P = 128
+PACK = 4
+TOKENS = 16 * 256
+K = P * PACK
+N_IN = 256
+COLS = PACK * N_IN
+BANK_COLS = 512
+HALVES = COLS // BANK_COLS
+TILES = TOKENS // P
+GROUP = 4
+GROUPS = TILES // GROUP
+TILES_PER_BANK = 2
+TILES_PER_STORE = 2
+
+FLOPS = 2 * TOKENS * K * COLS
+BYTES = TOKENS * K * 2 + 4 * P * N_IN * 2 + TOKENS * COLS * 4
+
+HAMILTON = (
+    ((0, 1.0), (1, -1.0), (2, -1.0), (3, -1.0)),
+    ((1, 1.0), (0, 1.0), (3, 1.0), (2, -1.0)),
+    ((2, 1.0), (3, -1.0), (0, 1.0), (1, 1.0)),
+    ((3, 1.0), (2, 1.0), (1, -1.0), (0, 1.0)),
+)
+
+
+def tile_quaternionlinear_t_kernel(tc, q_in, r_weight, i_weight, j_weight, k_weight, grad_out, out):
+    nc = tc.nc
+
+    g_rows = grad_out.flatten_outer_dims().rearrange("(p j) k -> p j k", j=TILES)
+    out_rows = out.flatten_outer_dims().rearrange("(p j) c -> p j c", j=TILES)
+
+    with ExitStack() as ctx:
+        keep = ctx.enter_context(tc.tile_pool(name="keep", bufs=1))
+        g_pool = ctx.enter_context(tc.tile_pool(name="g", bufs=GROUPS))
+        grouped_pool = ctx.enter_context(tc.tile_pool(name="grouped", bufs=2))
+        mx_pool = ctx.enter_context(tc.tile_pool(name="mx", bufs=3))
+        out_pool = ctx.enter_context(tc.tile_pool(name="result", bufs=6))
+        xt_pool = ctx.enter_context(tc.psum_pool(name="xt", bufs=2))
+        acc_pool = ctx.enter_context(tc.psum_pool(name="acc", bufs=6))
+
+        raw = keep.tile([P, PACK, N_IN], BF16)
+        for comp, weight in enumerate((r_weight, i_weight, j_weight, k_weight)):
+            nc.sync.dma_start(out=raw[:, comp, :], in_=weight)
+        g_tiles = []
+        for grp in range(GROUPS):
+            g_sb = g_pool.tile([P, GROUP * K], BF16)
+            nc.sync.dma_start(
+                out=g_sb[:].rearrange("p (j k) -> p j k", j=GROUP),
+                in_=g_rows[:, grp * GROUP : (grp + 1) * GROUP, :],
+            )
+            g_tiles.append(g_sb)
+
+        identity = keep.tile([P, P], F32)
+        make_identity(nc, identity[:])
+
+        signed = keep.tile([P, PACK * PACK, N_IN], BF16)
+        for c in range(PACK):
+            for d in range(PACK):
+                comp, sign = HAMILTON[d][c]
+                nc.vector.tensor_scalar_mul(out=signed[:, PACK * c + d, :], in0=raw[:, comp, :], scalar1=sign)
+        wt = keep.tile([P, N_IN, PACK * PACK], BF16, align_bytes=64)
+        w_codes = keep.tile([P, COLS], U32, align_bytes=64)
+        w_scales = keep.tile([P, COLS], U8, align_bytes=64)
+        n_half = N_IN // HALVES
+        for half in range(HALVES):
+            n_range = slice(half * n_half, (half + 1) * n_half)
+            col_range = slice(half * BANK_COLS, (half + 1) * BANK_COLS)
+            nc.vector.tensor_copy(out=wt[:, n_range, :], in_=signed[:, :, n_range].rearrange("m s n -> m n s"))
+            nc.vector.quantize_mx(
+                out=w_codes[:, col_range].bitcast(E4M3_X4),
+                scales=w_scales[:, col_range],
+                in_=wt[:, n_range, :].rearrange("m n s -> m (n s)"),
+            )
+
+        grouped_tiles = {}
+        mx_tiles = {}
+
+        def transpose_group(grp):
+            words = g_tiles[grp][:].bitcast(F32).rearrange("p (j m u) -> p j u m", j=GROUP, u=2)
+            grouped = grouped_pool.tile([P, GROUP * P * PACK], BF16, align_bytes=64)
+            grouped_words = grouped[:].bitcast(F32).rearrange("m (j t u) -> m j t u", j=GROUP, u=2)
+            for first in range(0, GROUP, TILES_PER_BANK):
+                xt = xt_pool.tile([P, TILES_PER_BANK, 2, P], F32)
+                for a in range(TILES_PER_BANK):
+                    for u in range(2):
+                        nc.tensor.transpose(xt[:, a, u, :], words[:, first + a, u, :], identity[:])
+                nc.scalar.copy(
+                    out=grouped_words[:, first : first + TILES_PER_BANK, :, :],
+                    in_=xt[:].rearrange("m a u t -> m a t u"),
+                )
+            grouped_tiles[grp] = grouped
+
+        def quantise_group(grp):
+            g_codes = mx_pool.tile([P, GROUP * P], U32, align_bytes=64)
+            g_scales = mx_pool.tile([P, GROUP * P], U8, align_bytes=64)
+            nc.vector.quantize_mx(out=g_codes[:].bitcast(E5M2_X4), scales=g_scales[:], in_=grouped_tiles[grp][:])
+            mx_tiles[grp] = (g_codes, g_scales)
+
+        def multiply_group(grp):
+            g_codes, g_scales = mx_tiles[grp]
+            result = out_pool.tile([P, GROUP, COLS], F32)
+            for j in range(GROUP):
+                tokens = slice(j * P, (j + 1) * P)
+                for half in range(HALVES):
+                    col_range = slice(half * BANK_COLS, (half + 1) * BANK_COLS)
+                    acc = acc_pool.tile([P, BANK_COLS], F32)
+                    nc.tensor.matmul_mx(
+                        out=acc[:],
+                        lhsT=g_codes[:, tokens].bitcast(E5M2_X4),
+                        lhsT_scale=g_scales[:, tokens],
+                        rhs=w_codes[:, col_range].bitcast(E4M3_X4),
+                        rhs_scale=w_scales[:, col_range],
+                        start=True,
+                        stop=True,
+                    )
+                    if half == 0:
+                        nc.scalar.copy(out=result[:, j, col_range], in_=acc[:])
+                    else:
+                        nc.vector.tensor_copy(out=result[:, j, col_range], in_=acc[:])
+                if (j + 1) % TILES_PER_STORE == 0:
+                    first = j + 1 - TILES_PER_STORE
+                    nc.sync.dma_start(
+                        out=out_rows[:, grp * GROUP + first : grp * GROUP + j + 1, :],
+                        in_=result[:, first : j + 1, :],
+                    )
+
+        for grp in range(-2, GROUPS):
+            if 0 <= grp + 1 < GROUPS:
+                quantise_group(grp + 1)
+            if grp + 2 < GROUPS:
+                transpose_group(grp + 2)
+            if grp >= 0:
+                multiply_group(grp)

@@ -22,7 +22,7 @@ TILES = TOKENS // P
 GROUP = 4
 GROUPS = TILES // GROUP
 TILES_PER_BANK = 2
-TILES_PER_STORE = 2
+N_PASS = BANK_COLS // PACK
 
 FLOPS = 2 * TOKENS * K * COLS
 BYTES = TOKENS * K * 2 + 4 * P * N_IN * 2 + TOKENS * COLS * 4
@@ -50,9 +50,10 @@ def tile_quaternionlinear_t_kernel(tc, q_in, r_weight, i_weight, j_weight, k_wei
         xt_pool = ctx.enter_context(tc.psum_pool(name="xt", bufs=2))
         acc_pool = ctx.enter_context(tc.psum_pool(name="acc", bufs=6))
 
-        raw = keep.tile([P, PACK, N_IN], BF16)
-        for comp, weight in enumerate((r_weight, i_weight, j_weight, k_weight)):
-            nc.sync.dma_start(out=raw[:, comp, :], in_=weight)
+        signed = keep.tile([P, PACK, PACK, N_IN], BF16)
+        for d, weight in enumerate((r_weight, i_weight, j_weight, k_weight)):
+            assert HAMILTON[d][0] == (d, 1.0)
+            nc.sync.dma_start(out=signed[:, 0, d, :], in_=weight)
         g_tiles = []
         for grp in range(GROUPS):
             g_sb = g_pool.tile([P, GROUP * K], BF16)
@@ -65,23 +66,21 @@ def tile_quaternionlinear_t_kernel(tc, q_in, r_weight, i_weight, j_weight, k_wei
         identity = keep.tile([P, P], F32)
         make_identity(nc, identity[:])
 
-        signed = keep.tile([P, PACK * PACK, N_IN], BF16)
-        for c in range(PACK):
+        for c in range(1, PACK):
             for d in range(PACK):
                 comp, sign = HAMILTON[d][c]
-                nc.vector.tensor_scalar_mul(out=signed[:, PACK * c + d, :], in0=raw[:, comp, :], scalar1=sign)
-        wt = keep.tile([P, N_IN, PACK * PACK], BF16, align_bytes=64)
+                nc.vector.tensor_scalar_mul(out=signed[:, c, d, :], in0=signed[:, 0, comp, :], scalar1=sign)
+        wt = keep.tile([P, HALVES, PACK, N_PASS, PACK], BF16, align_bytes=64)
         w_codes = keep.tile([P, COLS], U32, align_bytes=64)
         w_scales = keep.tile([P, COLS], U8, align_bytes=64)
-        n_half = N_IN // HALVES
         for half in range(HALVES):
-            n_range = slice(half * n_half, (half + 1) * n_half)
+            n_range = slice(half * N_PASS, (half + 1) * N_PASS)
             col_range = slice(half * BANK_COLS, (half + 1) * BANK_COLS)
-            nc.vector.tensor_copy(out=wt[:, n_range, :], in_=signed[:, :, n_range].rearrange("m s n -> m n s"))
+            nc.vector.tensor_copy(out=wt[:, half, :, :, :], in_=signed[:, :, :, n_range].rearrange("m c d n -> m c n d"))
             nc.vector.quantize_mx(
                 out=w_codes[:, col_range].bitcast(E4M3_X4),
                 scales=w_scales[:, col_range],
-                in_=wt[:, n_range, :].rearrange("m n s -> m (n s)"),
+                in_=wt[:, half, :, :, :].rearrange("m c n d -> m (c n d)"),
             )
 
         grouped_tiles = {}
@@ -125,16 +124,13 @@ def tile_quaternionlinear_t_kernel(tc, q_in, r_weight, i_weight, j_weight, k_wei
                         start=True,
                         stop=True,
                     )
+                    in_out_order = acc[:].rearrange("t (c n) -> t n c", c=PACK)
+                    destination = result[:, j, col_range].rearrange("t (n c) -> t n c", c=PACK)
                     if half == 0:
-                        nc.scalar.copy(out=result[:, j, col_range], in_=acc[:])
+                        nc.scalar.copy(out=destination, in_=in_out_order)
                     else:
-                        nc.vector.tensor_copy(out=result[:, j, col_range], in_=acc[:])
-                if (j + 1) % TILES_PER_STORE == 0:
-                    first = j + 1 - TILES_PER_STORE
-                    nc.sync.dma_start(
-                        out=out_rows[:, grp * GROUP + first : grp * GROUP + j + 1, :],
-                        in_=result[:, first : j + 1, :],
-                    )
+                        nc.vector.tensor_copy(out=destination, in_=in_out_order)
+            nc.sync.dma_start(out=out_rows[:, grp * GROUP : (grp + 1) * GROUP, :], in_=result[:])
 
         for grp in range(-2, GROUPS):
             if 0 <= grp + 1 < GROUPS:

@@ -22,6 +22,7 @@ TILES = TOKENS // P
 GROUP = 4
 GROUPS = TILES // GROUP
 TILES_PER_BANK = 2
+C_SPLIT = PACK // 2
 N_PASS = BANK_COLS // PACK
 
 FLOPS = 2 * TOKENS * K * COLS
@@ -76,7 +77,9 @@ def tile_quaternionlinear_t_kernel(tc, q_in, r_weight, i_weight, j_weight, k_wei
         for half in range(HALVES):
             n_range = slice(half * N_PASS, (half + 1) * N_PASS)
             col_range = slice(half * BANK_COLS, (half + 1) * BANK_COLS)
-            nc.vector.tensor_copy(out=wt[:, half, :, :, :], in_=signed[:, :, :, n_range].rearrange("m c d n -> m c n d"))
+            side_by_side = signed[:, :, :, n_range].rearrange("m c d n -> m c n d")
+            nc.scalar.copy(out=wt[:, half, :C_SPLIT, :, :], in_=side_by_side[:, :C_SPLIT, :, :])
+            nc.vector.tensor_copy(out=wt[:, half, C_SPLIT:, :, :], in_=side_by_side[:, C_SPLIT:, :, :])
             nc.vector.quantize_mx(
                 out=w_codes[:, col_range].bitcast(E4M3_X4),
                 scales=w_scales[:, col_range],
@@ -130,7 +133,10 @@ def tile_quaternionlinear_t_kernel(tc, q_in, r_weight, i_weight, j_weight, k_wei
                         nc.scalar.copy(out=destination, in_=in_out_order)
                     else:
                         nc.vector.tensor_copy(out=destination, in_=in_out_order)
-            nc.sync.dma_start(out=out_rows[:, grp * GROUP : (grp + 1) * GROUP, :], in_=result[:])
+                if grp == 0:
+                    nc.sync.dma_start(out=out_rows[:, j, :], in_=result[:, j, :])
+            if grp > 0:
+                nc.sync.dma_start(out=out_rows[:, grp * GROUP : (grp + 1) * GROUP, :], in_=result[:])
 
         for grp in range(-2, GROUPS):
             if 0 <= grp + 1 < GROUPS:

@@ -21,6 +21,7 @@ HALVES = COLS // BANK_COLS
 TILES = TOKENS // P
 GROUP = 4
 GROUPS = TILES // GROUP
+EARLY_GROUPS = 2
 TILES_PER_BANK = 2
 C_SPLIT = PACK // 2
 N_PASS = BANK_COLS // PACK
@@ -51,6 +52,8 @@ def tile_quaternionlinear_t_kernel(tc, q_in, r_weight, i_weight, j_weight, k_wei
         xt_pool = ctx.enter_context(tc.psum_pool(name="xt", bufs=2))
         acc_pool = ctx.enter_context(tc.psum_pool(name="acc", bufs=6))
 
+        ctx.enter_context(tc.manual_schedule())
+
         signed = keep.tile([P, PACK, PACK, N_IN], BF16)
         for d, weight in enumerate((r_weight, i_weight, j_weight, k_weight)):
             assert HAMILTON[d][0] == (d, 1.0)
@@ -66,6 +69,9 @@ def tile_quaternionlinear_t_kernel(tc, q_in, r_weight, i_weight, j_weight, k_wei
 
         identity = keep.tile([P, P], F32)
         make_identity(nc, identity[:])
+
+        table_warmer = keep.tile([P, 1], F32)
+        nc.scalar.copy(out=table_warmer[:], in_=identity[:, 0:1])
 
         for c in range(1, PACK):
             for d in range(PACK):
@@ -133,15 +139,15 @@ def tile_quaternionlinear_t_kernel(tc, q_in, r_weight, i_weight, j_weight, k_wei
                         nc.scalar.copy(out=destination, in_=in_out_order)
                     else:
                         nc.vector.tensor_copy(out=destination, in_=in_out_order)
-                if grp == 0:
-                    nc.sync.dma_start(out=out_rows[:, j, :], in_=result[:, j, :])
-            if grp > 0:
+                if grp < EARLY_GROUPS:
+                    nc.sync.dma_start(out=out_rows[:, grp * GROUP + j, :], in_=result[:, j, :])
+            if grp >= EARLY_GROUPS:
                 nc.sync.dma_start(out=out_rows[:, grp * GROUP : (grp + 1) * GROUP, :], in_=result[:])
 
-        for grp in range(-2, GROUPS):
-            if 0 <= grp + 1 < GROUPS:
+        transpose_group(0)
+        quantise_group(0)
+        for grp in range(GROUPS):
+            if grp + 1 < GROUPS:
+                transpose_group(grp + 1)
                 quantise_group(grp + 1)
-            if grp + 2 < GROUPS:
-                transpose_group(grp + 2)
-            if grp >= 0:
-                multiply_group(grp)
+            multiply_group(grp)

@@ -19,11 +19,12 @@ COLS = PACK * N_IN
 BANK_COLS = 512
 HALVES = COLS // BANK_COLS
 TILES = TOKENS // P
+PSUM_BANKS = 8
+TILES_PER_BANK = 2
 GROUP = 4
 GROUPS = TILES // GROUP
-EARLY_GROUPS = 2
-TILES_PER_BANK = 2
-C_SPLIT = PACK // 2
+UNIT_TILES = (2, 2) + (GROUP,) * (GROUPS - 1)
+EARLY_TILES = 2 * GROUP
 N_PASS = BANK_COLS // PACK
 
 FLOPS = 2 * TOKENS * K * COLS
@@ -36,34 +37,43 @@ HAMILTON = (
     ((3, 1.0), (2, 1.0), (1, -1.0), (0, 1.0)),
 )
 
+SLOT_HOLDS = ((1, -1.0), (0, 1.0), (1, 1.0), (3, -1.0), (2, 1.0), (3, 1.0), (2, -1.0), (3, -1.0))
+SLOTS = 10
+CORNERS = ((1, 3, 1), (0, 3, 1), (6, -5, -1), (7, -5, -1))
+assert all(
+    SLOT_HOLDS[CORNERS[c][0] + CORNERS[c][1] * (d // 2) + CORNERS[c][2] * (d % 2)] == HAMILTON[d][c]
+    for c in range(PACK)
+    for d in range(PACK)
+)
+
 
 def tile_quaternionlinear_t_kernel(tc, q_in, r_weight, i_weight, j_weight, k_weight, grad_out, out):
     nc = tc.nc
 
     g_rows = grad_out.flatten_outer_dims().rearrange("(p j) k -> p j k", j=TILES)
     out_rows = out.flatten_outer_dims().rearrange("(p j) c -> p j c", j=TILES)
+    units = len(UNIT_TILES)
+    first_tile = [sum(UNIT_TILES[:u]) for u in range(units)]
 
     with ExitStack() as ctx:
         keep = ctx.enter_context(tc.tile_pool(name="keep", bufs=1))
-        g_pool = ctx.enter_context(tc.tile_pool(name="g", bufs=GROUPS))
-        grouped_pool = ctx.enter_context(tc.tile_pool(name="grouped", bufs=2))
+        g_pool = ctx.enter_context(tc.tile_pool(name="g", bufs=units))
+        grouped_pool = ctx.enter_context(tc.tile_pool(name="grouped", bufs=3))
         mx_pool = ctx.enter_context(tc.tile_pool(name="mx", bufs=3))
-        out_pool = ctx.enter_context(tc.tile_pool(name="result", bufs=6))
-        xt_pool = ctx.enter_context(tc.psum_pool(name="xt", bufs=2))
-        acc_pool = ctx.enter_context(tc.psum_pool(name="acc", bufs=6))
+        out_pool = ctx.enter_context(tc.tile_pool(name="result", bufs=GROUPS))
+        psum = ctx.enter_context(tc.psum_pool(name="psum", bufs=PSUM_BANKS))
 
         ctx.enter_context(tc.manual_schedule())
 
-        signed = keep.tile([P, PACK, PACK, N_IN], BF16)
-        for d, weight in enumerate((r_weight, i_weight, j_weight, k_weight)):
-            assert HAMILTON[d][0] == (d, 1.0)
-            nc.sync.dma_start(out=signed[:, 0, d, :], in_=weight)
+        slots = keep.tile([P, SLOTS, N_IN], BF16)
+        for comp, weight in enumerate((r_weight, i_weight, j_weight, k_weight)):
+            nc.sync.dma_start(out=slots[:, SLOT_HOLDS.index((comp, 1.0)), :], in_=weight)
         g_tiles = []
-        for grp in range(GROUPS):
-            g_sb = g_pool.tile([P, GROUP * K], BF16)
+        for u in range(units):
+            g_sb = g_pool.tile([P, UNIT_TILES[u] * K], BF16, tag="g")
             nc.sync.dma_start(
-                out=g_sb[:].rearrange("p (j k) -> p j k", j=GROUP),
-                in_=g_rows[:, grp * GROUP : (grp + 1) * GROUP, :],
+                out=g_sb[:].rearrange("p (j k) -> p j k", j=UNIT_TILES[u]),
+                in_=g_rows[:, first_tile[u] : first_tile[u] + UNIT_TILES[u], :],
             )
             g_tiles.append(g_sb)
 
@@ -73,81 +83,117 @@ def tile_quaternionlinear_t_kernel(tc, q_in, r_weight, i_weight, j_weight, k_wei
         table_warmer = keep.tile([P, 1], F32)
         nc.scalar.copy(out=table_warmer[:], in_=identity[:, 0:1])
 
-        for c in range(1, PACK):
-            for d in range(PACK):
-                comp, sign = HAMILTON[d][c]
-                nc.vector.tensor_scalar_mul(out=signed[:, c, d, :], in0=signed[:, 0, comp, :], scalar1=sign)
+        xt_tiles = {}
+        grouped_tiles = {}
+        mx_tiles = {}
+        results = {}
+
+        def transpose_unit(u):
+            words = g_tiles[u][:].bitcast(F32).rearrange("p (j m w) -> p j w m", j=UNIT_TILES[u], w=2)
+            xt_tiles[u] = []
+            for first in range(0, UNIT_TILES[u], TILES_PER_BANK):
+                xt = psum.tile([P, TILES_PER_BANK, 2, P], F32, tag="bank")
+                for e in range(TILES_PER_BANK):
+                    for w in range(2):
+                        nc.tensor.transpose(xt[:, e, w, :], words[:, first + e, w, :], identity[:])
+                xt_tiles[u].append(xt)
+
+        def copy_out_unit(u):
+            grouped = grouped_pool.tile([P, UNIT_TILES[u] * P * PACK], BF16, tag="grouped", align_bytes=64)
+            grouped_words = grouped[:].bitcast(F32).rearrange("m (j t w) -> m j t w", j=UNIT_TILES[u], w=2)
+            for b, xt in enumerate(xt_tiles[u]):
+                nc.scalar.copy(
+                    out=grouped_words[:, b * TILES_PER_BANK : (b + 1) * TILES_PER_BANK, :, :],
+                    in_=xt[:].rearrange("m e w t -> m e t w"),
+                )
+            grouped_tiles[u] = grouped
+
+        def quantise_unit(u):
+            g_codes = mx_pool.tile([P, UNIT_TILES[u] * P], U32, tag="codes", align_bytes=64)
+            g_scales = mx_pool.tile([P, UNIT_TILES[u] * P], U8, tag="scales", align_bytes=64)
+            nc.vector.quantize_mx(out=g_codes[:].bitcast(E5M2_X4), scales=g_scales[:], in_=grouped_tiles[u][:])
+            mx_tiles[u] = (g_codes, g_scales)
+
+        def multiply_tile(u, j):
+            g_codes, g_scales = mx_tiles[u]
+            tile_index = first_tile[u] + j
+            grp, place = divmod(tile_index, GROUP)
+            if place == 0:
+                result = out_pool.tile([P, GROUP, COLS], F32, tag="result")
+                results[grp] = result
+            result = results[grp]
+            tokens = slice(j * P, (j + 1) * P)
+            for half in range(HALVES):
+                col_range = slice(half * BANK_COLS, (half + 1) * BANK_COLS)
+                acc = psum.tile([P, BANK_COLS], F32, tag="bank")
+                nc.tensor.matmul_mx(
+                    out=acc[:],
+                    lhsT=g_codes[:, tokens].bitcast(E5M2_X4),
+                    lhsT_scale=g_scales[:, tokens],
+                    rhs=w_codes[:, col_range].bitcast(E4M3_X4),
+                    rhs_scale=w_scales[:, col_range],
+                    start=True,
+                    stop=True,
+                )
+                in_out_order = acc[:].rearrange("t (c n) -> t n c", c=PACK)
+                destination = result[:, place, col_range].rearrange("t (n c) -> t n c", c=PACK)
+                if half == 0:
+                    nc.scalar.copy(out=destination, in_=in_out_order)
+                else:
+                    nc.vector.tensor_copy(out=destination, in_=in_out_order)
+            if tile_index < EARLY_TILES:
+                nc.sync.dma_start(out=out_rows[:, tile_index, :], in_=result[:, place, :])
+            elif place == GROUP - 1:
+                nc.sync.dma_start(out=out_rows[:, grp * GROUP : (grp + 1) * GROUP, :], in_=result[:])
+
+        nc.vector.tensor_scalar_mul(out=slots[:, 6:8, :], in0=slots[:, 4:6, :], scalar1=-1.0)
+        nc.vector.tensor_scalar_mul(out=slots[:, 0:4:3, :], in0=slots[:, 2:6:3, :], scalar1=-1.0)
+        transpose_unit(0)
+        transpose_unit(1)
+
+        rows_of_3 = slots[:, 0:6, :].rearrange("m (a s) n -> m a s n", a=2)
+        rows_of_5 = slots[:].rearrange("m (a s) n -> m a s n", a=2)
+        entries = (
+            rows_of_3[:, :, 1:3, :],
+            rows_of_3[:, :, 0:2, :],
+            rows_of_5[:, ::-1, 1::-1, :],
+            rows_of_5[:, ::-1, 2:0:-1, :],
+        )
         wt = keep.tile([P, HALVES, PACK, N_PASS, PACK], BF16, align_bytes=64)
         w_codes = keep.tile([P, COLS], U32, align_bytes=64)
         w_scales = keep.tile([P, COLS], U8, align_bytes=64)
-        for half in range(HALVES):
-            n_range = slice(half * N_PASS, (half + 1) * N_PASS)
+
+        def lay_side_by_side(half, c, copy):
+            copy(
+                out=wt[:, half, c, :, :].rearrange("m n (a b) -> m n a b", a=2),
+                in_=entries[c][:, :, :, half * N_PASS : (half + 1) * N_PASS].rearrange("m a b n -> m n a b"),
+            )
+
+        def quantise_weights(half):
             col_range = slice(half * BANK_COLS, (half + 1) * BANK_COLS)
-            side_by_side = signed[:, :, :, n_range].rearrange("m c d n -> m c n d")
-            nc.scalar.copy(out=wt[:, half, :C_SPLIT, :, :], in_=side_by_side[:, :C_SPLIT, :, :])
-            nc.vector.tensor_copy(out=wt[:, half, C_SPLIT:, :, :], in_=side_by_side[:, C_SPLIT:, :, :])
             nc.vector.quantize_mx(
                 out=w_codes[:, col_range].bitcast(E4M3_X4),
                 scales=w_scales[:, col_range],
                 in_=wt[:, half, :, :, :].rearrange("m c n d -> m (c n d)"),
             )
 
-        grouped_tiles = {}
-        mx_tiles = {}
+        for half in range(HALVES):
+            lay_side_by_side(half, 0, nc.scalar.copy)
+            lay_side_by_side(half, 1, nc.vector.tensor_copy)
+            lay_side_by_side(half, 2, nc.vector.tensor_copy)
+            lay_side_by_side(half, 3, nc.scalar.copy)
+            copy_out_unit(half)
+        quantise_weights(0)
+        quantise_unit(0)
+        quantise_weights(1)
+        quantise_unit(1)
 
-        def transpose_group(grp):
-            words = g_tiles[grp][:].bitcast(F32).rearrange("p (j m u) -> p j u m", j=GROUP, u=2)
-            grouped = grouped_pool.tile([P, GROUP * P * PACK], BF16, align_bytes=64)
-            grouped_words = grouped[:].bitcast(F32).rearrange("m (j t u) -> m j t u", j=GROUP, u=2)
-            for first in range(0, GROUP, TILES_PER_BANK):
-                xt = xt_pool.tile([P, TILES_PER_BANK, 2, P], F32)
-                for a in range(TILES_PER_BANK):
-                    for u in range(2):
-                        nc.tensor.transpose(xt[:, a, u, :], words[:, first + a, u, :], identity[:])
-                nc.scalar.copy(
-                    out=grouped_words[:, first : first + TILES_PER_BANK, :, :],
-                    in_=xt[:].rearrange("m a u t -> m a t u"),
-                )
-            grouped_tiles[grp] = grouped
-
-        def quantise_group(grp):
-            g_codes = mx_pool.tile([P, GROUP * P], U32, align_bytes=64)
-            g_scales = mx_pool.tile([P, GROUP * P], U8, align_bytes=64)
-            nc.vector.quantize_mx(out=g_codes[:].bitcast(E5M2_X4), scales=g_scales[:], in_=grouped_tiles[grp][:])
-            mx_tiles[grp] = (g_codes, g_scales)
-
-        def multiply_group(grp):
-            g_codes, g_scales = mx_tiles[grp]
-            result = out_pool.tile([P, GROUP, COLS], F32)
-            for j in range(GROUP):
-                tokens = slice(j * P, (j + 1) * P)
-                for half in range(HALVES):
-                    col_range = slice(half * BANK_COLS, (half + 1) * BANK_COLS)
-                    acc = acc_pool.tile([P, BANK_COLS], F32)
-                    nc.tensor.matmul_mx(
-                        out=acc[:],
-                        lhsT=g_codes[:, tokens].bitcast(E5M2_X4),
-                        lhsT_scale=g_scales[:, tokens],
-                        rhs=w_codes[:, col_range].bitcast(E4M3_X4),
-                        rhs_scale=w_scales[:, col_range],
-                        start=True,
-                        stop=True,
-                    )
-                    in_out_order = acc[:].rearrange("t (c n) -> t n c", c=PACK)
-                    destination = result[:, j, col_range].rearrange("t (n c) -> t n c", c=PACK)
-                    if half == 0:
-                        nc.scalar.copy(out=destination, in_=in_out_order)
-                    else:
-                        nc.vector.tensor_copy(out=destination, in_=in_out_order)
-                if grp < EARLY_GROUPS:
-                    nc.sync.dma_start(out=out_rows[:, grp * GROUP + j, :], in_=result[:, j, :])
-            if grp >= EARLY_GROUPS:
-                nc.sync.dma_start(out=out_rows[:, grp * GROUP : (grp + 1) * GROUP, :], in_=result[:])
-
-        transpose_group(0)
-        quantise_group(0)
-        for grp in range(GROUPS):
-            if grp + 1 < GROUPS:
-                transpose_group(grp + 1)
-                quantise_group(grp + 1)
-            multiply_group(grp)
+        for u in range(units):
+            if u + 2 < units:
+                transpose_unit(u + 2)
+            for j in range(UNIT_TILES[u]):
+                if j == UNIT_TILES[u] - 1 and 2 <= u + 1 < units:
+                    quantise_unit(u + 1)
+                multiply_tile(u, j)
+                if j == 1 and u + 2 < units:
+                    copy_out_unit(u + 2)

@@ -20,6 +20,7 @@ BANK_COLS = 512
 HALVES = COLS // BANK_COLS
 TILES = TOKENS // P
 PSUM_BANKS = 8
+DMA_ALIGN = 256
 TILES_PER_BANK = 2
 GROUP = 4
 GROUPS = TILES // GROUP
@@ -65,12 +66,12 @@ def tile_quaternionlinear_t_kernel(tc, q_in, r_weight, i_weight, j_weight, k_wei
 
         ctx.enter_context(tc.manual_schedule())
 
-        slots = keep.tile([P, SLOTS, N_IN], BF16)
+        slots = keep.tile([P, SLOTS, N_IN], BF16, align_bytes=DMA_ALIGN)
         for comp, weight in enumerate((r_weight, i_weight, j_weight, k_weight)):
             nc.sync.dma_start(out=slots[:, SLOT_HOLDS.index((comp, 1.0)), :], in_=weight)
         g_tiles = []
         for u in range(units):
-            g_sb = g_pool.tile([P, UNIT_TILES[u] * K], BF16, tag="g")
+            g_sb = g_pool.tile([P, UNIT_TILES[u] * K], BF16, tag="g", align_bytes=DMA_ALIGN)
             nc.sync.dma_start(
                 out=g_sb[:].rearrange("p (j k) -> p j k", j=UNIT_TILES[u]),
                 in_=g_rows[:, first_tile[u] : first_tile[u] + UNIT_TILES[u], :],
@@ -119,7 +120,7 @@ def tile_quaternionlinear_t_kernel(tc, q_in, r_weight, i_weight, j_weight, k_wei
             tile_index = first_tile[u] + j
             grp, place = divmod(tile_index, GROUP)
             if place == 0:
-                result = out_pool.tile([P, GROUP, COLS], F32, tag="result")
+                result = out_pool.tile([P, GROUP, COLS], F32, tag="result", align_bytes=DMA_ALIGN)
                 results[grp] = result
             result = results[grp]
             tokens = slice(j * P, (j + 1) * P)

@@ -25,7 +25,7 @@ TILES_PER_BANK = 2
 GROUP = 4
 GROUPS = TILES // GROUP
 UNIT_TILES = (2, 2) + (GROUP,) * (GROUPS - 1)
-EARLY_TILES = 2 * GROUP
+STORE_TILES = (1,) * (2 * GROUP) + (2, 2) + (GROUP,) * (GROUPS - 3)
 N_PASS = BANK_COLS // PACK
 
 FLOPS = 2 * TOKENS * K * COLS
@@ -55,6 +55,7 @@ def tile_quaternionlinear_t_kernel(tc, q_in, r_weight, i_weight, j_weight, k_wei
     out_rows = out.flatten_outer_dims().rearrange("(p j) c -> p j c", j=TILES)
     units = len(UNIT_TILES)
     first_tile = [sum(UNIT_TILES[:u]) for u in range(units)]
+    store_ends = [sum(STORE_TILES[: s + 1]) for s in range(len(STORE_TILES))]
 
     with ExitStack() as ctx:
         keep = ctx.enter_context(tc.tile_pool(name="keep", bufs=1))
@@ -142,10 +143,12 @@ def tile_quaternionlinear_t_kernel(tc, q_in, r_weight, i_weight, j_weight, k_wei
                     nc.scalar.copy(out=destination, in_=in_out_order)
                 else:
                     nc.vector.tensor_copy(out=destination, in_=in_out_order)
-            if tile_index < EARLY_TILES:
-                nc.sync.dma_start(out=out_rows[:, tile_index, :], in_=result[:, place, :])
-            elif place == GROUP - 1:
-                nc.sync.dma_start(out=out_rows[:, grp * GROUP : (grp + 1) * GROUP, :], in_=result[:])
+            if tile_index + 1 in store_ends:
+                count = STORE_TILES[store_ends.index(tile_index + 1)]
+                nc.sync.dma_start(
+                    out=out_rows[:, tile_index + 1 - count : tile_index + 1, :],
+                    in_=result[:, place + 1 - count : place + 1, :],
+                )
 
         nc.vector.tensor_scalar_mul(out=slots[:, 6:8, :], in0=slots[:, 4:6, :], scalar1=-1.0)
         nc.vector.tensor_scalar_mul(out=slots[:, 0:4:3, :], in0=slots[:, 2:6:3, :], scalar1=-1.0)

@@ -104,7 +104,8 @@ def tile_quaternionlinear_t_kernel(tc, q_in, r_weight, i_weight, j_weight, k_wei
             grouped = grouped_pool.tile([P, UNIT_TILES[u] * P * PACK], BF16, tag="grouped", align_bytes=64)
             grouped_words = grouped[:].bitcast(F32).rearrange("m (j t w) -> m j t w", j=UNIT_TILES[u], w=2)
             for b, xt in enumerate(xt_tiles[u]):
-                nc.scalar.copy(
+                copy = nc.vector.tensor_copy if b == 1 and u % 2 == 0 else nc.scalar.copy
+                copy(
                     out=grouped_words[:, b * TILES_PER_BANK : (b + 1) * TILES_PER_BANK, :, :],
                     in_=xt[:].rearrange("m e w t -> m e t w"),
                 )
@@ -181,12 +182,16 @@ def tile_quaternionlinear_t_kernel(tc, q_in, r_weight, i_weight, j_weight, k_wei
                 in_=wt[:, half, :, :, :].rearrange("m c n d -> m (c n d)"),
             )
 
-        for half in range(HALVES):
-            lay_side_by_side(half, 0, nc.scalar.copy)
-            lay_side_by_side(half, 1, nc.vector.tensor_copy)
-            lay_side_by_side(half, 2, nc.vector.tensor_copy)
-            lay_side_by_side(half, 3, nc.scalar.copy)
-            copy_out_unit(half)
+        lay_side_by_side(0, 0, nc.scalar.copy)
+        lay_side_by_side(0, 1, nc.vector.tensor_copy)
+        lay_side_by_side(0, 2, nc.vector.tensor_copy)
+        lay_side_by_side(0, 3, nc.vector.tensor_copy)
+        copy_out_unit(0)
+        lay_side_by_side(1, 0, nc.scalar.copy)
+        lay_side_by_side(1, 1, nc.vector.tensor_copy)
+        lay_side_by_side(1, 2, nc.vector.tensor_copy)
+        lay_side_by_side(1, 3, nc.scalar.copy)
+        copy_out_unit(1)
         quantise_weights(0)
         quantise_unit(0)
         quantise_weights(1)

@@ -20,6 +20,8 @@ BANK_COLS = 512
 HALVES = COLS // BANK_COLS
 TILES = TOKENS // P
 PSUM_BANKS = 8
+WARM_BEFORE_LOADS = 5
+WARM_BETWEEN = 2
 DMA_ALIGN = 256
 TILES_PER_BANK = 2
 GROUP = 4
@@ -151,10 +153,19 @@ def tile_quaternionlinear_t_kernel(tc, q_in, r_weight, i_weight, j_weight, k_wei
                     in_=result[:, place + 1 - count : place + 1, :],
                 )
 
+        def keep_tensor_busy(operand, width, times):
+            unread = psum.tile([P, BANK_COLS], F32, tag="bank")
+            for repeat in range(times):
+                nc.tensor.matmul(
+                    out=unread[:, :width], lhsT=operand[:, :P], rhs=operand[:, :width], start=True, stop=True
+                )
+
         nc.vector.tensor_scalar_mul(out=slots[:, 6:8, :], in0=slots[:, 4:6, :], scalar1=-1.0)
         nc.vector.tensor_scalar_mul(out=slots[:, 0:4:3, :], in0=slots[:, 2:6:3, :], scalar1=-1.0)
+        keep_tensor_busy(identity, P, WARM_BEFORE_LOADS)
         transpose_unit(0)
         transpose_unit(1)
+        keep_tensor_busy(identity, P, WARM_BETWEEN)
 
         rows_of_3 = slots[:, 0:6, :].rearrange("m (a s) n -> m a s n", a=2)
         rows_of_5 = slots[:].rearrange("m (a s) n -> m a s n", a=2)
@@ -196,9 +207,11 @@ def tile_quaternionlinear_t_kernel(tc, q_in, r_weight, i_weight, j_weight, k_wei
         quantise_unit(0)
         quantise_weights(1)
         quantise_unit(1)
+        transpose_unit(2)
+        keep_tensor_busy(grouped_tiles[0], BANK_COLS, WARM_BETWEEN)
 
         for u in range(units):
-            if u + 2 < units:
+            if 0 < u < units - 2:
                 transpose_unit(u + 2)
             for j in range(UNIT_TILES[u]):
                 if j == UNIT_TILES[u] - 1 and 2 <= u + 1 < units:

@@ -27,6 +27,7 @@ TILES_PER_BANK = 2
 GROUP = 4
 GROUPS = TILES // GROUP
 UNIT_TILES = (2, 2) + (GROUP,) * (GROUPS - 1)
+LOAD_TILES = (2, 2, 4, 8, 16)
 STORE_TILES = (1,) * (2 * GROUP) + (2, 2) + (GROUP,) * (GROUPS - 3)
 N_PASS = BANK_COLS // PACK
 
@@ -61,7 +62,6 @@ def tile_quaternionlinear_t_kernel(tc, q_in, r_weight, i_weight, j_weight, k_wei
 
     with ExitStack() as ctx:
         keep = ctx.enter_context(tc.tile_pool(name="keep", bufs=1))
-        g_pool = ctx.enter_context(tc.tile_pool(name="g", bufs=units))
         grouped_pool = ctx.enter_context(tc.tile_pool(name="grouped", bufs=3))
         mx_pool = ctx.enter_context(tc.tile_pool(name="mx", bufs=3))
         out_pool = ctx.enter_context(tc.tile_pool(name="result", bufs=GROUPS))
@@ -72,14 +72,14 @@ def tile_quaternionlinear_t_kernel(tc, q_in, r_weight, i_weight, j_weight, k_wei
         slots = keep.tile([P, SLOTS, N_IN], BF16, align_bytes=DMA_ALIGN)
         for comp, weight in enumerate((r_weight, i_weight, j_weight, k_weight)):
             nc.sync.dma_start(out=slots[:, SLOT_HOLDS.index((comp, 1.0)), :], in_=weight)
-        g_tiles = []
-        for u in range(units):
-            g_sb = g_pool.tile([P, UNIT_TILES[u] * K], BF16, tag="g", align_bytes=DMA_ALIGN)
-            nc.sync.dma_start(
-                out=g_sb[:].rearrange("p (j k) -> p j k", j=UNIT_TILES[u]),
-                in_=g_rows[:, first_tile[u] : first_tile[u] + UNIT_TILES[u], :],
-            )
-            g_tiles.append(g_sb)
+        g_words = {}
+        loaded = 0
+        for count in LOAD_TILES:
+            g_sb = keep.tile([P, count, K], BF16, name="g_from_%d" % loaded, align_bytes=DMA_ALIGN)
+            nc.sync.dma_start(out=g_sb[:], in_=g_rows[:, loaded : loaded + count, :])
+            for j in range(count):
+                g_words[loaded + j] = g_sb[:, j, :].bitcast(F32)
+            loaded += count
 
         identity = keep.tile([P, P], F32)
         make_identity(nc, identity[:])
@@ -93,13 +93,13 @@ def tile_quaternionlinear_t_kernel(tc, q_in, r_weight, i_weight, j_weight, k_wei
         results = {}
 
         def transpose_unit(u):
-            words = g_tiles[u][:].bitcast(F32).rearrange("p (j m w) -> p j w m", j=UNIT_TILES[u], w=2)
             xt_tiles[u] = []
             for first in range(0, UNIT_TILES[u], TILES_PER_BANK):
                 xt = psum.tile([P, TILES_PER_BANK, 2, P], F32, tag="bank")
                 for e in range(TILES_PER_BANK):
+                    words = g_words[first_tile[u] + first + e].rearrange("p (m w) -> p w m", w=2)
                     for w in range(2):
-                        nc.tensor.transpose(xt[:, e, w, :], words[:, first + e, w, :], identity[:])
+                        nc.tensor.transpose(xt[:, e, w, :], words[:, w, :], identity[:])
                 xt_tiles[u].append(xt)
 
         def copy_out_unit(u):

from contextlib import ExitStack

import concourse.mybir as mybir
from concourse.masks import make_identity

F32 = mybir.dt.float32
BF16 = mybir.dt.bfloat16
U32 = mybir.dt.uint32
U8 = mybir.dt.uint8
E4M3_X4 = mybir.dt.float8_e4m3fn_x4
E5M2_X4 = mybir.dt.float8_e5m2_x4

P = 128
PACK = 4
TOKENS = 16 * 256
K = P * PACK
N_IN = 256
COLS = PACK * N_IN
BANK_COLS = 512
HALVES = COLS // BANK_COLS
TILES = TOKENS // P
PSUM_BANKS = 8
WARM_BEFORE_LOADS = 5
WARM_BETWEEN = 2
DMA_ALIGN = 256
TILES_PER_BANK = 2
GROUP = 4
GROUPS = TILES // GROUP
UNIT_TILES = (2, 2) + (GROUP,) * (GROUPS - 1)
LOAD_TILES = (2, 2, 4, 8, 16)
STORE_TILES = (1,) * (2 * GROUP) + (2, 2) + (GROUP,) * (GROUPS - 3)
N_PASS = BANK_COLS // PACK

FLOPS = 2 * TOKENS * K * COLS
BYTES = TOKENS * K * 2 + 4 * P * N_IN * 2 + TOKENS * COLS * 4

HAMILTON = (
    ((0, 1.0), (1, -1.0), (2, -1.0), (3, -1.0)),
    ((1, 1.0), (0, 1.0), (3, 1.0), (2, -1.0)),
    ((2, 1.0), (3, -1.0), (0, 1.0), (1, 1.0)),
    ((3, 1.0), (2, 1.0), (1, -1.0), (0, 1.0)),
)

SLOT_HOLDS = ((1, -1.0), (0, 1.0), (1, 1.0), (3, -1.0), (2, 1.0), (3, 1.0), (2, -1.0), (3, -1.0))
SLOTS = 10
CORNERS = ((1, 3, 1), (0, 3, 1), (6, -5, -1), (7, -5, -1))
assert all(
    SLOT_HOLDS[CORNERS[c][0] + CORNERS[c][1] * (d // 2) + CORNERS[c][2] * (d % 2)] == HAMILTON[d][c]
    for c in range(PACK)
    for d in range(PACK)
)


def tile_quaternionlinear_t_kernel(tc, q_in, r_weight, i_weight, j_weight, k_weight, grad_out, out):
    nc = tc.nc

    g_rows = grad_out.flatten_outer_dims().rearrange("(p j) k -> p j k", j=TILES)
    out_rows = out.flatten_outer_dims().rearrange("(p j) c -> p j c", j=TILES)
    units = len(UNIT_TILES)
    first_tile = [sum(UNIT_TILES[:u]) for u in range(units)]
    store_ends = [sum(STORE_TILES[: s + 1]) for s in range(len(STORE_TILES))]

    with ExitStack() as ctx:
        keep = ctx.enter_context(tc.tile_pool(name="keep", bufs=1))
        grouped_pool = ctx.enter_context(tc.tile_pool(name="grouped", bufs=3))
        mx_pool = ctx.enter_context(tc.tile_pool(name="mx", bufs=3))
        out_pool = ctx.enter_context(tc.tile_pool(name="result", bufs=GROUPS))
        psum = ctx.enter_context(tc.psum_pool(name="psum", bufs=PSUM_BANKS))

        ctx.enter_context(tc.manual_schedule())

        slots = keep.tile([P, SLOTS, N_IN], BF16, align_bytes=DMA_ALIGN)
        for comp, weight in enumerate((r_weight, i_weight, j_weight, k_weight)):
            nc.sync.dma_start(out=slots[:, SLOT_HOLDS.index((comp, 1.0)), :], in_=weight)
        g_words = {}
        loaded = 0
        for count in LOAD_TILES:
            g_sb = keep.tile([P, count, K], BF16, name="g_from_%d" % loaded, align_bytes=DMA_ALIGN)
            nc.sync.dma_start(out=g_sb[:], in_=g_rows[:, loaded : loaded + count, :])
            for j in range(count):
                g_words[loaded + j] = g_sb[:, j, :].bitcast(F32)
            loaded += count

        identity = keep.tile([P, P], F32)
        make_identity(nc, identity[:])

        table_warmer = keep.tile([P, 1], F32)
        nc.scalar.copy(out=table_warmer[:], in_=identity[:, 0:1])

        xt_tiles = {}
        grouped_tiles = {}
        mx_tiles = {}
        results = {}

        def transpose_unit(u):
            xt_tiles[u] = []
            for first in range(0, UNIT_TILES[u], TILES_PER_BANK):
                xt = psum.tile([P, TILES_PER_BANK, 2, P], F32, tag="bank")
                for e in range(TILES_PER_BANK):
                    words = g_words[first_tile[u] + first + e].rearrange("p (m w) -> p w m", w=2)
                    for w in range(2):
                        nc.tensor.transpose(xt[:, e, w, :], words[:, w, :], identity[:])
                xt_tiles[u].append(xt)

        def copy_out_unit(u):
            grouped = grouped_pool.tile([P, UNIT_TILES[u] * P * PACK], BF16, tag="grouped", align_bytes=64)
            grouped_words = grouped[:].bitcast(F32).rearrange("m (j t w) -> m j t w", j=UNIT_TILES[u], w=2)
            for b, xt in enumerate(xt_tiles[u]):
                copy = nc.vector.tensor_copy if b == 1 and u % 2 == 0 else nc.scalar.copy
                copy(
                    out=grouped_words[:, b * TILES_PER_BANK : (b + 1) * TILES_PER_BANK, :, :],
                    in_=xt[:].rearrange("m e w t -> m e t w"),
                )
            grouped_tiles[u] = grouped

        def quantise_unit(u):
            g_codes = mx_pool.tile([P, UNIT_TILES[u] * P], U32, tag="codes", align_bytes=64)
            g_scales = mx_pool.tile([P, UNIT_TILES[u] * P], U8, tag="scales", align_bytes=64)
            nc.vector.quantize_mx(out=g_codes[:].bitcast(E5M2_X4), scales=g_scales[:], in_=grouped_tiles[u][:])
            mx_tiles[u] = (g_codes, g_scales)

        def multiply_tile(u, j):
            g_codes, g_scales = mx_tiles[u]
            tile_index = first_tile[u] + j
            grp, place = divmod(tile_index, GROUP)
            if place == 0:
                result = out_pool.tile([P, GROUP, COLS], F32, tag="result", align_bytes=DMA_ALIGN)
                results[grp] = result
            result = results[grp]
            tokens = slice(j * P, (j + 1) * P)
            for half in range(HALVES):
                col_range = slice(half * BANK_COLS, (half + 1) * BANK_COLS)
                acc = psum.tile([P, BANK_COLS], F32, tag="bank")
                nc.tensor.matmul_mx(
                    out=acc[:],
                    lhsT=g_codes[:, tokens].bitcast(E5M2_X4),
                    lhsT_scale=g_scales[:, tokens],
                    rhs=w_codes[:, col_range].bitcast(E4M3_X4),
                    rhs_scale=w_scales[:, col_range],
                    start=True,
                    stop=True,
                )
                in_out_order = acc[:].rearrange("t (c n) -> t n c", c=PACK)
                destination = result[:, place, col_range].rearrange("t (n c) -> t n c", c=PACK)
                if half == 0:
                    nc.scalar.copy(out=destination, in_=in_out_order)
                else:
                    nc.vector.tensor_copy(out=destination, in_=in_out_order)
            if tile_index + 1 in store_ends:
                count = STORE_TILES[store_ends.index(tile_index + 1)]
                nc.sync.dma_start(
                    out=out_rows[:, tile_index + 1 - count : tile_index + 1, :],
                    in_=result[:, place + 1 - count : place + 1, :],
                )

        def keep_tensor_busy(operand, width, times):
            unread = psum.tile([P, BANK_COLS], F32, tag="bank")
            for repeat in range(times):
                nc.tensor.matmul(
                    out=unread[:, :width], lhsT=operand[:, :P], rhs=operand[:, :width], start=True, stop=True
                )

        nc.vector.tensor_scalar_mul(out=slots[:, 6:8, :], in0=slots[:, 4:6, :], scalar1=-1.0)
        nc.vector.tensor_scalar_mul(out=slots[:, 0:4:3, :], in0=slots[:, 2:6:3, :], scalar1=-1.0)
        keep_tensor_busy(identity, P, WARM_BEFORE_LOADS)
        transpose_unit(0)
        transpose_unit(1)
        keep_tensor_busy(identity, P, WARM_BETWEEN)

        rows_of_3 = slots[:, 0:6, :].rearrange("m (a s) n -> m a s n", a=2)
        rows_of_5 = slots[:].rearrange("m (a s) n -> m a s n", a=2)
        entries = (
            rows_of_3[:, :, 1:3, :],
            rows_of_3[:, :, 0:2, :],
            rows_of_5[:, ::-1, 1::-1, :],
            rows_of_5[:, ::-1, 2:0:-1, :],
        )
        wt = keep.tile([P, HALVES, PACK, N_PASS, PACK], BF16, align_bytes=64)
        w_codes = keep.tile([P, COLS], U32, align_bytes=64)
        w_scales = keep.tile([P, COLS], U8, align_bytes=64)

        def lay_side_by_side(half, c, copy):
            copy(
                out=wt[:, half, c, :, :].rearrange("m n (a b) -> m n a b", a=2),
                in_=entries[c][:, :, :, half * N_PASS : (half + 1) * N_PASS].rearrange("m a b n -> m n a b"),
            )

        def quantise_weights(half):
            col_range = slice(half * BANK_COLS, (half + 1) * BANK_COLS)
            nc.vector.quantize_mx(
                out=w_codes[:, col_range].bitcast(E4M3_X4),
                scales=w_scales[:, col_range],
                in_=wt[:, half, :, :, :].rearrange("m c n d -> m (c n d)"),
            )

        lay_side_by_side(0, 0, nc.scalar.copy)
        lay_side_by_side(0, 1, nc.vector.tensor_copy)
        lay_side_by_side(0, 2, nc.vector.tensor_copy)
        lay_side_by_side(0, 3, nc.vector.tensor_copy)
        copy_out_unit(0)
        lay_side_by_side(1, 0, nc.scalar.copy)
        lay_side_by_side(1, 1, nc.vector.tensor_copy)
        lay_side_by_side(1, 2, nc.vector.tensor_copy)
        lay_side_by_side(1, 3, nc.scalar.copy)
        copy_out_unit(1)
        quantise_weights(0)
        quantise_unit(0)
        quantise_weights(1)
        quantise_unit(1)
        transpose_unit(2)
        keep_tensor_busy(grouped_tiles[0], BANK_COLS, WARM_BETWEEN)

        for u in range(units):
            if 0 < u < units - 2:
                transpose_unit(u + 2)
            for j in range(UNIT_TILES[u]):
                if j == UNIT_TILES[u] - 1 and 2 <= u + 1 < units:
                    quantise_unit(u + 1)
                multiply_tile(u, j)
                if j == 1 and u + 2 < units:
                    copy_out_unit(u + 2)
